import numpy as np
import ml_dtypes


def mxq(x, axis, fmt="e4m3"):
    dtype, down = {"e4m3": (ml_dtypes.float8_e4m3fn, 7), "e5m2": (ml_dtypes.float8_e5m2, 14)}[fmt]
    v = np.moveaxis(np.asarray(x, np.float32).astype(ml_dtypes.bfloat16).astype(np.float64), axis, -1)
    blocks = v.reshape(v.shape[:-1] + (-1, 32))
    amax = np.abs(blocks).max(-1, keepdims=True)
    byte = np.maximum(np.where(amax > 0, np.frexp(amax)[1] - 1 + 127, 0) - down, 1)
    scale = np.exp2(byte - 127.0)
    codes = (blocks / scale).astype(np.float32).astype(dtype).astype(np.float64)
    return np.moveaxis((codes * scale).reshape(v.shape), -1, axis)


WIDE = False


def mx_kscale(k):
    if not WIDE:
        return np.ones(k)
    levels = np.array([10, -10, 5, -5, 0])
    a = np.random.permutation(np.resize(levels, k // 512 * 4)).reshape(k // 512, 4)
    idx = np.arange(k)
    return np.exp2(a[idx // 512, idx % 128 // 32])


BF16 = ml_dtypes.bfloat16


def bf(x):
    return np.asarray(x, np.float32).astype(BF16)


def f64(x):
    return np.asarray(x).astype(np.float64)


B, S, D, H, F, QB = 4, 1024, 512, 4, 1536, 512
HD = D // H
EPS = 1e-5


def setup_inputs():
    s = mx_kscale(D)
    return {"x": bf(np.random.standard_normal((B, S, D))),
            "rms_w": bf((1.0 + 0.1 * np.random.standard_normal(D)) * s),
            "w_qkv": bf(np.random.standard_normal((3 * D, D)) * 1.5 / np.sqrt(D) / s[None, :])}


def reference(x, rms_w, w_qkv):
    xf = f64(x)
    xn = xf / np.sqrt(np.mean(xf * xf, axis=-1, keepdims=True) + EPS) * f64(rms_w)
    y = mxq(xn, 2, "e4m3") @ mxq(f64(w_qkv), 1, "e4m3").T
    return y.reshape(B, S, 3, H, HD).transpose(2, 0, 3, 1, 4)

@@ -1,0 +1,200 @@
+from contextlib import ExitStack
+
+import concourse.mybir as mybir
+from concourse.masks import make_identity
+
+F32 = mybir.dt.float32
+BF16 = mybir.dt.bfloat16
+U32 = mybir.dt.uint32
+U8 = mybir.dt.uint8
+FP8X4 = mybir.dt.float8_e4m3fn_x4
+ACT = mybir.ActivationFunctionType
+ALU = mybir.AluOpType
+
+P = 128
+PACK = 4
+B, S, D = 4, 1024, 512
+C, H, HD = 3, 4, 128
+EPS = 1e-5
+T = S // P
+N = H * HD
+PAIRS_PER_BATCH = T // 2
+
+FLOPS = 2 * B * S * C * N * D
+
+
+def tile_transformerblock_pa_t_kernel(tc, x, rms_w, w_qkv, out):
+    nc = tc.nc
+    with ExitStack() as stack:
+        keep = stack.enter_context(tc.tile_pool(name="keep", bufs=1))
+        squares = stack.enter_context(tc.tile_pool(name="squares", bufs=4))
+        scaled_pool = stack.enter_context(tc.tile_pool(name="scaled", bufs=8))
+        grouped_pool = stack.enter_context(tc.tile_pool(name="grouped", bufs=3))
+        w_grouped_pool = stack.enter_context(tc.tile_pool(name="w_grouped", bufs=2))
+        y_pool = stack.enter_context(tc.tile_pool(name="y", bufs=6))
+        flip_pool = stack.enter_context(tc.psum_pool(name="flip", bufs=4))
+        acc_pool = stack.enter_context(tc.psum_pool(name="acc", bufs=4))
+
+        ident = keep.tile([P, P], F32, name="ident")
+        eps = keep.tile([P, 1], F32, name="eps")
+        warm = keep.tile([P, 1], F32, name="warm")
+        gain = keep.tile([P, PACK], BF16, name="gain")
+        sumsq = keep.tile([P, B * T], F32, name="sumsq")
+        rinv = keep.tile([P, B * T], F32, name="rinv")
+        x_sb = [keep.tile([P, T * D], BF16, name="x%d" % b) for b in range(B)]
+        w_sb = [keep.tile([P, PACK * D], BF16, name="w%d" % c) for c in range(C)]
+        x_codes = keep.tile([P, B * T * P], U32, name="x_codes", align_bytes=64)
+        x_scales = keep.tile([P, B * T * P], U8, name="x_scales", align_bytes=64)
+        w_codes = keep.tile([P, C * N], U32, name="w_codes", align_bytes=64)
+        w_scales = keep.tile([P, C * N], U8, name="w_scales", align_bytes=64)
+        scaled = {}
+        flipped = {}
+        grouped = {}
+        y_tiles = {}
+
+        def load_x(b):
+            rows = x[b].rearrange("(p t) d -> p (t d)", t=T)
+            half = T * D // 2
+            for k in range(2):
+                nc.sync.dma_start(
+                    out=x_sb[b][:, k * half : (k + 1) * half], in_=rows[:, k * half : (k + 1) * half]
+                )
+
+        def load_w(c):
+            nc.sync.dma_start(
+                out=w_sb[c][:].rearrange("p (i k) -> p i k", k=D),
+                in_=w_qkv[c * N : (c + 1) * N, :].rearrange("(i p) k -> p i k", p=P),
+            )
+
+        def tile_of(g):
+            b, t = divmod(g, T)
+            return x_sb[b][:, t * D : (t + 1) * D]
+
+        def stats(q):
+            for g in (2 * q, 2 * q + 1):
+                sq = squares.tile([P, D], BF16, name="sq")
+                nc.scalar.activation(
+                    out=sq[:], in_=tile_of(g), func=ACT.Square, accum_out=sumsq[:, g : g + 1]
+                )
+            nc.scalar.activation(
+                out=rinv[:, 2 * q : 2 * q + 2],
+                in_=sumsq[:, 2 * q : 2 * q + 2],
+                func=ACT.Abs_reciprocal_sqrt,
+                bias=eps[:],
+                scale=1.0 / D,
+            )
+
+        def scale(q):
+            for g in (2 * q, 2 * q + 1):
+                scaled[g] = scaled_pool.tile([P, PACK, P], F32, name="scaled")
+                nc.gpsimd.tensor_scalar(
+                    out=scaled[g][:].rearrange("p (u e) q -> p u e q", e=2),
+                    in0=tile_of(g).rearrange("p (u q e) -> p u e q", u=2, e=2),
+                    scalar1=rinv[:, g : g + 1],
+                    scalar2=1.0,
+                    op0=ALU.mult,
+                    op1=ALU.mult,
+                )
+
+        def flip(q):
+            for g in (2 * q, 2 * q + 1):
+                flipped[g] = flip_pool.tile([P, PACK, P], F32, name="flipped")
+                for t in range(PACK):
+                    nc.tensor.transpose(flipped[g][:, t, :], scaled[g][:, t, :], ident[:])
+
+        def pack(q):
+            grouped[q] = grouped_pool.tile([P, 2 * P * PACK], BF16, name="grouped", align_bytes=64)
+            for k in range(2):
+                nc.vector.tensor_tensor(
+                    out=grouped[q][:, k * P * PACK : (k + 1) * P * PACK].rearrange(
+                        "p (r t) -> p r t", t=PACK
+                    ),
+                    in0=flipped[2 * q + k][:].rearrange("p t r -> p r t"),
+                    in1=gain[:].unsqueeze(1).to_broadcast([P, P, PACK]),
+                    op=ALU.mult,
+                )
+
+        def quantise(q):
+            cols = slice(2 * q * P, (2 * q + 2) * P)
+            nc.vector.quantize_mx(
+                out=x_codes[:, cols].bitcast(FP8X4), scales=x_scales[:, cols], in_=grouped[q][:]
+            )
+
+        def weights(c):
+            w_words = w_sb[c][:].bitcast(F32)
+            w_grouped = w_grouped_pool.tile([P, N * PACK], BF16, name="w_grouped", align_bytes=64)
+            g_words = w_grouped[:].bitcast(F32)
+            for k in range(2):
+                w_flipped = flip_pool.tile([P, PACK, P], F32, name="flipped")
+                for s in range(PACK):
+                    col = (k * PACK + s) * P
+                    nc.tensor.transpose(w_flipped[:, s, :], w_words[:, col : col + P], ident[:])
+                dst = g_words[:, k * N : (k + 1) * N].rearrange("p (i f u) -> p i f u", i=2, u=2)
+                src = w_flipped[:].rearrange("p (i u) f -> p i f u", u=2)
+                if k == 0:
+                    nc.vector.tensor_copy(out=dst, in_=src)
+                else:
+                    nc.scalar.copy(out=dst, in_=src)
+            cols = slice(c * N, (c + 1) * N)
+            nc.vector.quantize_mx(
+                out=w_codes[:, cols].bitcast(FP8X4), scales=w_scales[:, cols], in_=w_grouped[:]
+            )
+
+        def project(n):
+            b, rest = divmod(n, C * T)
+            c, t = divmod(rest, T)
+            tok = slice((b * T + t) * P, (b * T + t + 1) * P)
+            feat = slice(c * N, (c + 1) * N)
+            acc = acc_pool.tile([P, N], F32, name="acc")
+            nc.tensor.matmul_mx(
+                out=acc[:],
+                lhsT=x_codes[:, tok].bitcast(FP8X4),
+                lhsT_scale=x_scales[:, tok],
+                rhs=w_codes[:, feat].bitcast(FP8X4),
+                rhs_scale=w_scales[:, feat],
+                start=True,
+                stop=True,
+            )
+            if t == 0:
+                y_tiles[(b, c)] = y_pool.tile([P, H, T, HD], F32, name="y")
+            y = y_tiles[(b, c)]
+            src = acc[:].rearrange("p (h j) -> p h j", h=H)
+            if n % 2 == 0:
+                nc.scalar.copy(out=y[:, :, t, :], in_=src)
+            else:
+                nc.vector.tensor_copy(out=y[:, :, t, :], in_=src)
+            if t == T - 1:
+                nc.sync.dma_start(
+                    out=out[c, b].rearrange("h (p t) j -> p h (t j)", t=T),
+                    in_=y[:].rearrange("p h t j -> p h (t j)"),
+                )
+
+        nc.vector.memset(eps[:], EPS)
+        nc.scalar.activation(out=warm[:], in_=eps[:], func=ACT.Abs_reciprocal_sqrt)
+        make_identity(nc, ident[:])
+        nc.scalar.dma_start(
+            out=gain[:].rearrange("q (u e) -> q u e", e=2),
+            in_=rms_w.rearrange("(u q e) -> q u e", u=2, e=2),
+        )
+        load_x(0)
+        for c in range(C):
+            load_w(c)
+        for b in range(1, B):
+            load_x(b)
+
+        weights(0)
+        for b in range(B):
+            for j in range(PAIRS_PER_BATCH):
+                q = b * PAIRS_PER_BATCH + j
+                stats(q)
+                scale(q)
+                flip(q)
+                pack(q)
+                quantise(q)
+                project(b * C * T + 2 * j)
+                project(b * C * T + 2 * j + 1)
+            for c in range(1, C):
+                if b == 0:
+                    weights(c)
+                for t in range(T):
+                    project((b * C + c) * T + t)

@@ -159,7 +159,7 @@ def tile_transformerblock_pa_t_kernel(tc, x, rms_w, w_qkv, out):
                 y_tiles[(b, c)] = y_pool.tile([P, H, T, HD], F32, name="y")
             y = y_tiles[(b, c)]
             src = acc[:].rearrange("p (h j) -> p h j", h=H)
-            if n % 2 == 0:
+            if n % 3 != 2:
                 nc.scalar.copy(out=y[:, :, t, :], in_=src)
             else:
                 nc.vector.tensor_copy(out=y[:, :, t, :], in_=src)

@@ -87,7 +87,8 @@ def tile_transformerblock_pa_t_kernel(tc, x, rms_w, w_qkv, out):
         def scale(q):
             for g in (2 * q, 2 * q + 1):
                 scaled[g] = scaled_pool.tile([P, PACK, P], F32, name="scaled")
-                nc.gpsimd.tensor_scalar(
+                engine = nc.gpsimd if g % 2 == 0 else nc.vector
+                engine.tensor_scalar(
                     out=scaled[g][:].rearrange("p (u e) q -> p u e q", e=2),
                     in0=tile_of(g).rearrange("p (u q e) -> p u e q", u=2, e=2),
                     scalar1=rinv[:, g : g + 1],

from contextlib import ExitStack

import concourse.mybir as mybir
from concourse.masks import make_identity

F32 = mybir.dt.float32
BF16 = mybir.dt.bfloat16
U32 = mybir.dt.uint32
U8 = mybir.dt.uint8
FP8X4 = mybir.dt.float8_e4m3fn_x4
ACT = mybir.ActivationFunctionType
ALU = mybir.AluOpType

P = 128
PACK = 4
B, S, D = 4, 1024, 512
C, H, HD = 3, 4, 128
EPS = 1e-5
T = S // P
N = H * HD
PAIRS_PER_BATCH = T // 2

FLOPS = 2 * B * S * C * N * D


def tile_transformerblock_pa_t_kernel(tc, x, rms_w, w_qkv, out):
    nc = tc.nc
    with ExitStack() as stack:
        keep = stack.enter_context(tc.tile_pool(name="keep", bufs=1))
        squares = stack.enter_context(tc.tile_pool(name="squares", bufs=4))
        scaled_pool = stack.enter_context(tc.tile_pool(name="scaled", bufs=8))
        grouped_pool = stack.enter_context(tc.tile_pool(name="grouped", bufs=3))
        w_grouped_pool = stack.enter_context(tc.tile_pool(name="w_grouped", bufs=2))
        y_pool = stack.enter_context(tc.tile_pool(name="y", bufs=6))
        flip_pool = stack.enter_context(tc.psum_pool(name="flip", bufs=4))
        acc_pool = stack.enter_context(tc.psum_pool(name="acc", bufs=4))

        ident = keep.tile([P, P], F32, name="ident")
        eps = keep.tile([P, 1], F32, name="eps")
        warm = keep.tile([P, 1], F32, name="warm")
        gain = keep.tile([P, PACK], BF16, name="gain")
        sumsq = keep.tile([P, B * T], F32, name="sumsq")
        rinv = keep.tile([P, B * T], F32, name="rinv")
        x_sb = [keep.tile([P, T * D], BF16, name="x%d" % b) for b in range(B)]
        w_sb = [keep.tile([P, PACK * D], BF16, name="w%d" % c) for c in range(C)]
        x_codes = keep.tile([P, B * T * P], U32, name="x_codes", align_bytes=64)
        x_scales = keep.tile([P, B * T * P], U8, name="x_scales", align_bytes=64)
        w_codes = keep.tile([P, C * N], U32, name="w_codes", align_bytes=64)
        w_scales = keep.tile([P, C * N], U8, name="w_scales", align_bytes=64)
        scaled = {}
        flipped = {}
        grouped = {}
        y_tiles = {}

        def load_x(b):
            rows = x[b].rearrange("(p t) d -> p (t d)", t=T)
            half = T * D // 2
            for k in range(2):
                nc.sync.dma_start(
                    out=x_sb[b][:, k * half : (k + 1) * half], in_=rows[:, k * half : (k + 1) * half]
                )

        def load_w(c):
            nc.sync.dma_start(
                out=w_sb[c][:].rearrange("p (i k) -> p i k", k=D),
                in_=w_qkv[c * N : (c + 1) * N, :].rearrange("(i p) k -> p i k", p=P),
            )

        def tile_of(g):
            b, t = divmod(g, T)
            return x_sb[b][:, t * D : (t + 1) * D]

        def stats(q):
            for g in (2 * q, 2 * q + 1):
                sq = squares.tile([P, D], BF16, name="sq")
                nc.scalar.activation(
                    out=sq[:], in_=tile_of(g), func=ACT.Square, accum_out=sumsq[:, g : g + 1]
                )
            nc.scalar.activation(
                out=rinv[:, 2 * q : 2 * q + 2],
                in_=sumsq[:, 2 * q : 2 * q + 2],
                func=ACT.Abs_reciprocal_sqrt,
                bias=eps[:],
                scale=1.0 / D,
            )

        def scale(q):
            for g in (2 * q, 2 * q + 1):
                scaled[g] = scaled_pool.tile([P, PACK, P], F32, name="scaled")
                engine = nc.gpsimd if g % 2 == 0 else nc.vector
                engine.tensor_scalar(
                    out=scaled[g][:].rearrange("p (u e) q -> p u e q", e=2),
                    in0=tile_of(g).rearrange("p (u q e) -> p u e q", u=2, e=2),
                    scalar1=rinv[:, g : g + 1],
                    scalar2=1.0,
                    op0=ALU.mult,
                    op1=ALU.mult,
                )

        def flip(q):
            for g in (2 * q, 2 * q + 1):
                flipped[g] = flip_pool.tile([P, PACK, P], F32, name="flipped")
                for t in range(PACK):
                    nc.tensor.transpose(flipped[g][:, t, :], scaled[g][:, t, :], ident[:])

        def pack(q):
            grouped[q] = grouped_pool.tile([P, 2 * P * PACK], BF16, name="grouped", align_bytes=64)
            for k in range(2):
                nc.vector.tensor_tensor(
                    out=grouped[q][:, k * P * PACK : (k + 1) * P * PACK].rearrange(
                        "p (r t) -> p r t", t=PACK
                    ),
                    in0=flipped[2 * q + k][:].rearrange("p t r -> p r t"),
                    in1=gain[:].unsqueeze(1).to_broadcast([P, P, PACK]),
                    op=ALU.mult,
                )

        def quantise(q):
            cols = slice(2 * q * P, (2 * q + 2) * P)
            nc.vector.quantize_mx(
                out=x_codes[:, cols].bitcast(FP8X4), scales=x_scales[:, cols], in_=grouped[q][:]
            )

        def weights(c):
            w_words = w_sb[c][:].bitcast(F32)
            w_grouped = w_grouped_pool.tile([P, N * PACK], BF16, name="w_grouped", align_bytes=64)
            g_words = w_grouped[:].bitcast(F32)
            for k in range(2):
                w_flipped = flip_pool.tile([P, PACK, P], F32, name="flipped")
                for s in range(PACK):
                    col = (k * PACK + s) * P
                    nc.tensor.transpose(w_flipped[:, s, :], w_words[:, col : col + P], ident[:])
                dst = g_words[:, k * N : (k + 1) * N].rearrange("p (i f u) -> p i f u", i=2, u=2)
                src = w_flipped[:].rearrange("p (i u) f -> p i f u", u=2)
                if k == 0:
                    nc.vector.tensor_copy(out=dst, in_=src)
                else:
                    nc.scalar.copy(out=dst, in_=src)
            cols = slice(c * N, (c + 1) * N)
            nc.vector.quantize_mx(
                out=w_codes[:, cols].bitcast(FP8X4), scales=w_scales[:, cols], in_=w_grouped[:]
            )

        def project(n):
            b, rest = divmod(n, C * T)
            c, t = divmod(rest, T)
            tok = slice((b * T + t) * P, (b * T + t + 1) * P)
            feat = slice(c * N, (c + 1) * N)
            acc = acc_pool.tile([P, N], F32, name="acc")
            nc.tensor.matmul_mx(
                out=acc[:],
                lhsT=x_codes[:, tok].bitcast(FP8X4),
                lhsT_scale=x_scales[:, tok],
                rhs=w_codes[:, feat].bitcast(FP8X4),
                rhs_scale=w_scales[:, feat],
                start=True,
                stop=True,
            )
            if t == 0:
                y_tiles[(b, c)] = y_pool.tile([P, H, T, HD], F32, name="y")
            y = y_tiles[(b, c)]
            src = acc[:].rearrange("p (h j) -> p h j", h=H)
            if n % 3 != 2:
                nc.scalar.copy(out=y[:, :, t, :], in_=src)
            else:
                nc.vector.tensor_copy(out=y[:, :, t, :], in_=src)
            if t == T - 1:
                nc.sync.dma_start(
                    out=out[c, b].rearrange("h (p t) j -> p h (t j)", t=T),
                    in_=y[:].rearrange("p h t j -> p h (t j)"),
                )

        nc.vector.memset(eps[:], EPS)
        nc.scalar.activation(out=warm[:], in_=eps[:], func=ACT.Abs_reciprocal_sqrt)
        make_identity(nc, ident[:])
        nc.scalar.dma_start(
            out=gain[:].rearrange("q (u e) -> q u e", e=2),
            in_=rms_w.rearrange("(u q e) -> q u e", u=2, e=2),
        )
        load_x(0)
        for c in range(C):
            load_w(c)
        for b in range(1, B):
            load_x(b)

        weights(0)
        for b in range(B):
            for j in range(PAIRS_PER_BATCH):
                q = b * PAIRS_PER_BATCH + j
                stats(q)
                scale(q)
                flip(q)
                pack(q)
                quantise(q)
                project(b * C * T + 2 * j)
                project(b * C * T + 2 * j + 1)
            for c in range(1, C):
                if b == 0:
                    weights(c)
                for t in range(T):
                    project((b * C + c) * T + t)
